import numpy as np
import ml_dtypes


def mxq(x, axis, fmt="e4m3"):
    dtype, down = {"e4m3": (ml_dtypes.float8_e4m3fn, 7), "e5m2": (ml_dtypes.float8_e5m2, 14)}[fmt]
    v = np.moveaxis(np.asarray(x, np.float32).astype(ml_dtypes.bfloat16).astype(np.float64), axis, -1)
    blocks = v.reshape(v.shape[:-1] + (-1, 32))
    amax = np.abs(blocks).max(-1, keepdims=True)
    byte = np.maximum(np.where(amax > 0, np.frexp(amax)[1] - 1 + 127, 0) - down, 1)
    scale = np.exp2(byte - 127.0)
    codes = (blocks / scale).astype(np.float32).astype(dtype).astype(np.float64)
    return np.moveaxis((codes * scale).reshape(v.shape), -1, axis)


WIDE = False


def mx_kscale(k):
    if not WIDE:
        return np.ones(k)
    levels = np.array([10, -10, 5, -5, 0])
    if k % 512:
        return np.exp2(np.random.permutation(np.resize(levels, k // 32))).repeat(32)
    a = np.empty((k // 512, 16))
    for p in range(k // 512):
        a[p, :8] = np.random.permutation(np.resize(levels, 8))
        for g in range(8):
            far = levels[np.abs(levels - a[p, g]) >= 10]
            a[p, g + 8] = far[np.random.randint(len(far))]
    return np.exp2(a.ravel()).repeat(32)


BF16 = ml_dtypes.bfloat16


def bf(x):
    return np.asarray(x, np.float32).astype(BF16)


def f64(x):
    return np.asarray(x).astype(np.float64)


B, C, H, W, K = 4, 1024, 32, 32, 128
N = H * W
XS = 1.6 / C ** 0.25
CS = 0.4 / C ** 0.25


def draw0():
    s = mx_kscale(N)
    z = 1.3 * np.random.standard_normal((B, N, K)) + np.random.standard_normal((1, 1, K))
    a = np.exp(z - z.max(axis=-1, keepdims=True))
    a = a / a.sum(axis=-1, keepdims=True)
    feat = XS * (np.random.standard_normal((B, N, C)) + 0.4 * np.random.standard_normal((1, 1, C)))
    return {'assign': bf(a * s[None, :, None]),
            'xp': bf(feat / s[None, :, None]),
            'codebook': bf(np.random.standard_normal((K, C)) * CS / s.mean())}


def core(assign, xp, codebook):
    assign, xp, codebook = f64(assign), f64(xp), f64(codebook)
    a_sum = np.sum(assign, axis=1)
    e = (mxq(assign, 1, 'e4m3').transpose(0, 2, 1) @ mxq(xp, 1, 'e4m3')) - a_sum[:, :, None] * codebook[None]
    return e


def e4m3fn_bytes(y):
    return np.clip(np.asarray(y, np.float64), -448.0, 448.0).astype(np.float32).astype(ml_dtypes.float8_e4m3fn).view(np.uint8)


def e4m3fn_values(b):
    return np.asarray(b, np.uint8).view(ml_dtypes.float8_e4m3fn).astype(np.float64)


def setup_inputs():
    d = draw0()
    x0 = np.asarray(d['xp']).astype(np.float64)
    s = (np.max(np.abs(x0), axis=(0, 2), keepdims=True) / 448.0).astype(np.float32)
    out = {}
    for k, v in d.items():
        if k == 'xp':
            out['xp_bytes'] = e4m3fn_bytes(x0 / s.astype(np.float64))
            out['xp_scale'] = s
        else:
            out[k] = v
    return out


def reference(assign, xp_bytes, xp_scale, codebook):
    return core(assign, e4m3fn_values(xp_bytes) * xp_scale.astype(np.float64), codebook)

@@ -1,0 +1,211 @@
+from contextlib import ExitStack
+
+import concourse.mybir as mybir
+
+B, NPIX, C, K = 4, 1024, 1024, 128
+FLOPS = 2 * B * K * NPIX * C
+
+F32 = mybir.dt.float32
+BF16 = mybir.dt.bfloat16
+U32 = mybir.dt.uint32
+U8 = mybir.dt.uint8
+FP8 = mybir.dt.float8_e4m3fn
+FP8X4 = mybir.dt.float8_e4m3fn_x4
+COPY = mybir.ActivationFunctionType.Copy
+MULT = mybir.AluOpType.mult
+ADD = mybir.AluOpType.add
+
+P = 128
+PACK = 4
+K_PASS = P * PACK
+PASSES = NPIX // K_PASS
+
+WIDTHS = ((512, 512), (512, 512), (512, 512), (512, 256, 256))
+V_WIDENS = ((0, 1), (0, 2), (0, 3), (1, 3))
+S_INTERLEAVES = (13, 17)
+
+
+def tile_lvc_pb_kernel(tc, assign, xp_bytes, xp_scale, codebook, out):
+    nc = tc.nc
+
+    chunks = []
+    for b in range(B):
+        c0 = 0
+        for w in WIDTHS[b]:
+            for g in range(PASSES):
+                chunks.append((b, g, c0, w))
+            c0 += w
+    n_chunks = len(chunks)
+
+    with ExitStack() as ctx:
+        keep = ctx.enter_context(tc.tile_pool(name="keep", bufs=1))
+        widep = ctx.enter_context(tc.tile_pool(name="widep", bufs=6))
+        grpp = ctx.enter_context(tc.tile_pool(name="grpp", bufs=4))
+        outp = ctx.enter_context(tc.tile_pool(name="outp", bufs=3))
+        psum = ctx.enter_context(tc.psum_pool(name="psum", bufs=6))
+        psum1 = ctx.enter_context(tc.psum_pool(name="psum1", bufs=1))
+        ctx.enter_context(tc.manual_schedule())
+
+        xs = keep.tile([P, PASSES, PACK], F32, name="xs")
+        nc.scalar.dma_start(out=xs[:], in_=xp_scale[0, :, 0].rearrange("(g p t) -> p g t", p=P, t=PACK))
+
+        xbytes = []
+        for u in range(B * PASSES):
+            xb = keep.tile([P, PACK, C], U8, name="xbytes%d" % u)
+            xbytes.append(xb)
+
+        def load_bytes(b, g, t0, t1, c0, w):
+            src = xp_bytes[b, g * K_PASS:(g + 1) * K_PASS, c0:c0 + w].rearrange("(p t) c -> p t c", t=PACK)
+            nc.sync.dma_start(out=xbytes[b * PASSES + g][:, t0:t1, c0:c0 + w], in_=src[:, t0:t1, :])
+
+        a_raw = keep.tile([P, B * PASSES, PACK, K], BF16, name="a_raw")
+        a_view = assign.rearrange("b (g p t) k -> p (b g) (t k)", p=P, t=PACK)
+
+        def load_assign(n0, n1):
+            nc.sync.dma_start(out=a_raw[:, n0:n1, :, :].rearrange("p n t k -> p n (t k)"), in_=a_view[:, n0:n1, :])
+
+        for t in range(PACK):
+            load_bytes(0, 0, t, t + 1, 0, 512)
+        load_bytes(0, 1, 0, PACK, 0, 512)
+        load_assign(0, PASSES)
+        load_bytes(0, 0, 0, PACK, 512, 512)
+        load_bytes(0, 1, 0, PACK, 512, 512)
+        load_assign(PASSES, B * PASSES)
+        cb = keep.tile([P, C], BF16, name="cb")
+        nc.sync.dma_start(out=cb[:], in_=codebook)
+        for b in range(1, B):
+            for g in range(PASSES):
+                load_bytes(b, g, 0, PACK, 0, C)
+
+        neg_ones = keep.tile([P, 1], BF16, name="neg_ones")
+        nc.gpsimd.memset(neg_ones[:], -1.0)
+        warm_in = keep.tile([P, 1], F32, name="warm_in")
+        warm_out = keep.tile([P, 1], F32, name="warm_out")
+        nc.gpsimd.memset(warm_in[:], 0.0)
+        nc.scalar.activation(out=warm_out[:], in_=warm_in[:], func=COPY)
+
+        a_grouped = keep.tile([P, B * PASSES, K, PACK], BF16, name="a_grouped", align_bytes=64)
+        a_codes = keep.tile([P, B * PASSES * K], U32, name="a_codes", align_bytes=64)
+        a_planes = keep.tile([P, B * PASSES * K], U8, name="a_planes", align_bytes=64)
+        asum_ps = psum1.tile([P, B], F32, name="asum_ps")
+        neg_asum = keep.tile([P, B], F32, name="neg_asum")
+
+        wide = {}
+        grouped = {}
+        codes = {}
+        planes = {}
+        acc = {}
+
+        def widen(i):
+            b, g, c0, w = chunks[i]
+            wt = widep.tile([P, PACK, w], BF16, name="wide")
+            wide[i] = wt
+            for t in range(PACK):
+                src = xbytes[b * PASSES + g][:, t, c0:c0 + w].bitcast(FP8)
+                if (i, t) in V_WIDENS:
+                    nc.vector.tensor_scalar(out=wt[:, t, :], in0=src, scalar1=xs[:, g, t:t + 1], scalar2=None, op0=MULT)
+                else:
+                    nc.scalar.activation(out=wt[:, t, :], in_=src, func=COPY, scale=xs[:, g, t:t + 1])
+
+        def interleave(i):
+            w = chunks[i][3]
+            gt = grpp.tile([P, w, PACK], BF16, name="grouped", align_bytes=64)
+            grouped[i] = gt
+            src = wide[i][:].rearrange("p t c -> p c t")
+            if i in S_INTERLEAVES:
+                nc.scalar.copy(out=gt[:], in_=src)
+            else:
+                nc.vector.tensor_copy(out=gt[:], in_=src)
+
+        def quantize(i):
+            w = chunks[i][3]
+            xc = keep.tile([P, w], U32, name="codes%d" % i, align_bytes=64)
+            xpl = keep.tile([P, w], U8, name="planes%d" % i, align_bytes=64)
+            codes[i] = xc
+            planes[i] = xpl
+            nc.vector.quantize_mx(
+                out=xc[:].bitcast(FP8X4), scales=xpl[:], in_=grouped[i][:].rearrange("p c t -> p (c t)")
+            )
+
+        def multiply(i):
+            b, g, c0, w = chunks[i]
+            if g == 0:
+                acc_t = psum.tile([P, w], F32, name="acc")
+                acc[(b, c0)] = acc_t
+            a_cols = slice((b * PASSES + g) * K, (b * PASSES + g + 1) * K)
+            nc.tensor.matmul_mx(
+                out=acc[(b, c0)][:],
+                lhsT=a_codes[:, a_cols].bitcast(FP8X4),
+                lhsT_scale=a_planes[:, a_cols],
+                rhs=codes[i][:].bitcast(FP8X4),
+                rhs_scale=planes[i][:],
+                start=(g == 0),
+                stop=(g == PASSES - 1),
+            )
+
+        def finish(i):
+            b, g, c0, w = chunks[i]
+            ot = outp.tile([P, w], F32, name="ot")
+            nc.vector.scalar_tensor_tensor(
+                out=ot[:], in0=cb[:, c0:c0 + w], scalar=neg_asum[:, b:b + 1], in1=acc[(b, c0)][:], op0=MULT, op1=ADD
+            )
+            nc.sync.dma_start(out=out[b, :, c0:c0 + w], in_=ot[:])
+
+        def assign_sums(b0, b1):
+            for b in range(b0, b1):
+                for j in range(PASSES * PACK):
+                    nc.tensor.matmul(
+                        out=asum_ps[:, b:b + 1],
+                        lhsT=a_raw[:, b * PASSES + j // PACK, j % PACK, :],
+                        rhs=neg_ones[:],
+                        start=(j == 0),
+                        stop=(j == PASSES * PACK - 1),
+                    )
+
+        def assign_interleave(b):
+            n = slice(b * PASSES, (b + 1) * PASSES)
+            nc.vector.tensor_copy(out=a_grouped[:, n, :, :], in_=a_raw[:, n, :, :].rearrange("p n t k -> p n k t"))
+
+        def assign_quantize(b):
+            n = slice(b * PASSES, (b + 1) * PASSES)
+            cols = slice(b * PASSES * K, (b + 1) * PASSES * K)
+            nc.vector.quantize_mx(
+                out=a_codes[:, cols].bitcast(FP8X4),
+                scales=a_planes[:, cols],
+                in_=a_grouped[:, n, :, :].rearrange("p n k t -> p (n k t)"),
+            )
+
+        widen(0)
+        widen(1)
+        interleave(0)
+        assign_interleave(0)
+        assign_sums(0, 1)
+        assign_sums(1, B)
+        first_of_image = [i for i in range(n_chunks) if chunks[i][1:3] == (0, 0)]
+        closed = []
+        for i in range(n_chunks):
+            b = chunks[i][0]
+            if i + 1 in S_INTERLEAVES:
+                interleave(i + 1)
+            if i + 2 < n_chunks:
+                widen(i + 2)
+            if i + 1 < n_chunks and i + 1 not in S_INTERLEAVES:
+                interleave(i + 1)
+            if b + 1 < B and i == first_of_image[b] + 1:
+                assign_interleave(b + 1)
+            quantize(i)
+            if i == 0:
+                assign_quantize(0)
+                nc.vector.tensor_copy(out=neg_asum[:, 0:1], in_=asum_ps[:, 0:1])
+            if i == 2:
+                nc.vector.tensor_copy(out=neg_asum[:, 1:B], in_=asum_ps[:, 1:B])
+            if b + 1 < B and i == first_of_image[b] + 2:
+                assign_quantize(b + 1)
+            for j in closed:
+                finish(j)
+            closed = []
+            multiply(i)
+            if chunks[i][1] == PASSES - 1:
+                closed.append(i)
+        for j in closed:
+            finish(j)

@@ -21,8 +21,9 @@ K_PASS = P * PACK
 PASSES = NPIX // K_PASS
 
 WIDTHS = ((512, 512), (512, 512), (512, 512), (512, 256, 256))
-V_WIDENS = ((0, 1), (0, 2), (0, 3), (1, 3))
+V_WIDENS = ((0, 1), (0, 2), (0, 3), (1, 3), (4, 3), (6, 3), (8, 3), (10, 3))
 S_INTERLEAVES = (13, 17)
+RUN = 4
 
 
 def tile_lvc_pb_kernel(tc, assign, xp_bytes, xp_scale, codebook, out):
@@ -111,11 +112,13 @@ def tile_lvc_pb_kernel(tc, assign, xp_bytes, xp_scale, codebook, out):
             w = chunks[i][3]
             gt = grpp.tile([P, w, PACK], BF16, name="grouped", align_bytes=64)
             grouped[i] = gt
-            src = wide[i][:].rearrange("p t c -> p c t")
             if i in S_INTERLEAVES:
-                nc.scalar.copy(out=gt[:], in_=src)
+                nc.scalar.copy(out=gt[:], in_=wide[i][:].rearrange("p t c -> p c t"))
             else:
-                nc.vector.tensor_copy(out=gt[:], in_=src)
+                nc.vector.tensor_copy(
+                    out=gt[:].rearrange("p (c j) t -> p c t j", j=RUN),
+                    in_=wide[i][:].rearrange("p t (c j) -> p c t j", j=RUN),
+                )
 
         def quantize(i):
             w = chunks[i][3]
@@ -164,7 +167,11 @@ def tile_lvc_pb_kernel(tc, assign, xp_bytes, xp_scale, codebook, out):
 
         def assign_interleave(b):
             n = slice(b * PASSES, (b + 1) * PASSES)
-            nc.vector.tensor_copy(out=a_grouped[:, n, :, :], in_=a_raw[:, n, :, :].rearrange("p n t k -> p n k t"))
+            for m in range(b * PASSES, (b + 1) * PASSES):
+                nc.vector.tensor_copy(
+                    out=a_grouped[:, m, :, :].rearrange("p (k j) t -> p k t j", j=RUN),
+                    in_=a_raw[:, m, :, :].rearrange("p t (k j) -> p k t j", j=RUN),
+                )
 
         def assign_quantize(b):
             n = slice(b * PASSES, (b + 1) * PASSES)

@@ -20,9 +20,10 @@ PACK = 4
 K_PASS = P * PACK
 PASSES = NPIX // K_PASS
 
-WIDTHS = ((512, 512), (512, 512), (512, 512), (512, 256, 256))
-V_WIDENS = ((0, 1), (0, 2), (0, 3), (1, 3), (4, 3), (6, 3), (8, 3), (10, 3))
-S_INTERLEAVES = (13, 17)
+WIDTHS = ((1024,), (1024,), (1024,), (512, 256, 256))
+BANK = 512
+V_WIDENS = ((0, 1), (0, 2), (0, 3))
+S_INTERLEAVES = (7, 11)
 RUN = 4
 
 
@@ -40,9 +41,9 @@ def tile_lvc_pb_kernel(tc, assign, xp_bytes, xp_scale, codebook, out):
 
     with ExitStack() as ctx:
         keep = ctx.enter_context(tc.tile_pool(name="keep", bufs=1))
-        widep = ctx.enter_context(tc.tile_pool(name="widep", bufs=6))
-        grpp = ctx.enter_context(tc.tile_pool(name="grpp", bufs=4))
-        outp = ctx.enter_context(tc.tile_pool(name="outp", bufs=3))
+        widep = ctx.enter_context(tc.tile_pool(name="widep", bufs=4))
+        grpp = ctx.enter_context(tc.tile_pool(name="grpp", bufs=3))
+        outp = ctx.enter_context(tc.tile_pool(name="outp", bufs=4))
         psum = ctx.enter_context(tc.psum_pool(name="psum", bufs=6))
         psum1 = ctx.enter_context(tc.psum_pool(name="psum1", bufs=1))
         ctx.enter_context(tc.manual_schedule())
@@ -66,12 +67,9 @@ def tile_lvc_pb_kernel(tc, assign, xp_bytes, xp_scale, codebook, out):
             nc.sync.dma_start(out=a_raw[:, n0:n1, :, :].rearrange("p n t k -> p n (t k)"), in_=a_view[:, n0:n1, :])
 
         for t in range(PACK):
-            load_bytes(0, 0, t, t + 1, 0, 512)
-        load_bytes(0, 1, 0, PACK, 0, 512)
-        load_assign(0, PASSES)
-        load_bytes(0, 0, 0, PACK, 512, 512)
-        load_bytes(0, 1, 0, PACK, 512, 512)
-        load_assign(PASSES, B * PASSES)
+            load_bytes(0, 0, t, t + 1, 0, C)
+        load_bytes(0, 1, 0, PACK, 0, C)
+        load_assign(0, B * PASSES)
         cb = keep.tile([P, C], BF16, name="cb")
         nc.sync.dma_start(out=cb[:], in_=codebook)
         for b in range(1, B):
@@ -132,27 +130,31 @@ def tile_lvc_pb_kernel(tc, assign, xp_bytes, xp_scale, codebook, out):
 
         def multiply(i):
             b, g, c0, w = chunks[i]
-            if g == 0:
-                acc_t = psum.tile([P, w], F32, name="acc")
-                acc[(b, c0)] = acc_t
             a_cols = slice((b * PASSES + g) * K, (b * PASSES + g + 1) * K)
-            nc.tensor.matmul_mx(
-                out=acc[(b, c0)][:],
-                lhsT=a_codes[:, a_cols].bitcast(FP8X4),
-                lhsT_scale=a_planes[:, a_cols],
-                rhs=codes[i][:].bitcast(FP8X4),
-                rhs_scale=planes[i][:],
-                start=(g == 0),
-                stop=(g == PASSES - 1),
-            )
+            for d in range(0, w, BANK):
+                n = min(w, BANK)
+                if g == 0:
+                    acc_t = psum.tile([P, n], F32, name="acc")
+                    acc[(b, c0 + d)] = acc_t
+                nc.tensor.matmul_mx(
+                    out=acc[(b, c0 + d)][:],
+                    lhsT=a_codes[:, a_cols].bitcast(FP8X4),
+                    lhsT_scale=a_planes[:, a_cols],
+                    rhs=codes[i][:, d:d + n].bitcast(FP8X4),
+                    rhs_scale=planes[i][:, d:d + n],
+                    start=(g == 0),
+                    stop=(g == PASSES - 1),
+                )
 
         def finish(i):
             b, g, c0, w = chunks[i]
-            ot = outp.tile([P, w], F32, name="ot")
-            nc.vector.scalar_tensor_tensor(
-                out=ot[:], in0=cb[:, c0:c0 + w], scalar=neg_asum[:, b:b + 1], in1=acc[(b, c0)][:], op0=MULT, op1=ADD
-            )
-            nc.sync.dma_start(out=out[b, :, c0:c0 + w], in_=ot[:])
+            for d in range(c0, c0 + w, BANK):
+                n = min(w, BANK)
+                ot = outp.tile([P, n], F32, name="ot")
+                nc.vector.scalar_tensor_tensor(
+                    out=ot[:], in0=cb[:, d:d + n], scalar=neg_asum[:, b:b + 1], in1=acc[(b, d)][:], op0=MULT, op1=ADD
+                )
+                nc.sync.dma_start(out=out[b, :, d:d + n], in_=ot[:])
 
         def assign_sums(b0, b1):
             for b in range(b0, b1):
@@ -165,49 +167,31 @@ def tile_lvc_pb_kernel(tc, assign, xp_bytes, xp_scale, codebook, out):
                         stop=(j == PASSES * PACK - 1),
                     )
 
-        def assign_interleave(b):
-            n = slice(b * PASSES, (b + 1) * PASSES)
-            for m in range(b * PASSES, (b + 1) * PASSES):
-                nc.vector.tensor_copy(
-                    out=a_grouped[:, m, :, :].rearrange("p (k j) t -> p k t j", j=RUN),
-                    in_=a_raw[:, m, :, :].rearrange("p t (k j) -> p k t j", j=RUN),
-                )
+        def assign_interleave():
+            nc.vector.tensor_copy(out=a_grouped[:], in_=a_raw[:].rearrange("p n t k -> p n k t"))
 
-        def assign_quantize(b):
-            n = slice(b * PASSES, (b + 1) * PASSES)
-            cols = slice(b * PASSES * K, (b + 1) * PASSES * K)
+        def assign_quantize():
             nc.vector.quantize_mx(
-                out=a_codes[:, cols].bitcast(FP8X4),
-                scales=a_planes[:, cols],
-                in_=a_grouped[:, n, :, :].rearrange("p n k t -> p (n k t)"),
+                out=a_codes[:].bitcast(FP8X4), scales=a_planes[:], in_=a_grouped[:].rearrange("p n k t -> p (n k t)")
             )
 
         widen(0)
         widen(1)
         interleave(0)
-        assign_interleave(0)
-        assign_sums(0, 1)
-        assign_sums(1, B)
-        first_of_image = [i for i in range(n_chunks) if chunks[i][1:3] == (0, 0)]
+        assign_interleave()
+        assign_sums(0, B)
         closed = []
         for i in range(n_chunks):
-            b = chunks[i][0]
             if i + 1 in S_INTERLEAVES:
                 interleave(i + 1)
             if i + 2 < n_chunks:
                 widen(i + 2)
             if i + 1 < n_chunks and i + 1 not in S_INTERLEAVES:
                 interleave(i + 1)
-            if b + 1 < B and i == first_of_image[b] + 1:
-                assign_interleave(b + 1)
             quantize(i)
             if i == 0:
-                assign_quantize(0)
-                nc.vector.tensor_copy(out=neg_asum[:, 0:1], in_=asum_ps[:, 0:1])
-            if i == 2:
-                nc.vector.tensor_copy(out=neg_asum[:, 1:B], in_=asum_ps[:, 1:B])
-            if b + 1 < B and i == first_of_image[b] + 2:
-                assign_quantize(b + 1)
+                assign_quantize()
+                nc.vector.tensor_copy(out=neg_asum[:], in_=asum_ps[:])
             for j in closed:
                 finish(j)
             closed = []

@@ -24,7 +24,7 @@ WIDTHS = ((1024,), (1024,), (1024,), (512, 256, 256))
 BANK = 512
 V_WIDENS = ((0, 1), (0, 2), (0, 3))
 S_INTERLEAVES = (7, 11)
-RUN = 4
+RUN = 8
 
 
 def tile_lvc_pb_kernel(tc, assign, xp_bytes, xp_scale, codebook, out):
@@ -66,9 +66,9 @@ def tile_lvc_pb_kernel(tc, assign, xp_bytes, xp_scale, codebook, out):
         def load_assign(n0, n1):
             nc.sync.dma_start(out=a_raw[:, n0:n1, :, :].rearrange("p n t k -> p n (t k)"), in_=a_view[:, n0:n1, :])
 
-        for t in range(PACK):
-            load_bytes(0, 0, t, t + 1, 0, C)
-        load_bytes(0, 1, 0, PACK, 0, C)
+        for g in range(PASSES):
+            for t in range(PACK):
+                load_bytes(0, g, t, t + 1, 0, C)
         load_assign(0, B * PASSES)
         cb = keep.tile([P, C], BF16, name="cb")
         nc.sync.dma_start(out=cb[:], in_=codebook)

@@ -20,11 +20,15 @@ PACK = 4
 K_PASS = P * PACK
 PASSES = NPIX // K_PASS
 
-WIDTHS = ((1024,), (1024,), (1024,), (512, 256, 256))
-BANK = 512
+WIDTHS = (((1024,), (1024,)), ((1024,), (1024,)), ((1024,), (1024,)), ((1024,), (512, 256, 256)))
+
+RANGES = ((512, 512), (512, 512), (512, 512), (512, 256, 256))
+
 V_WIDENS = ((0, 1), (0, 2), (0, 3))
-S_INTERLEAVES = (7, 11)
-RUN = 8
+
+S_INTERLEAVES = (7, 9)
+
+RUN = 4
 
 
 def tile_lvc_pb_kernel(tc, assign, xp_bytes, xp_scale, codebook, out):
@@ -32,49 +36,57 @@ def tile_lvc_pb_kernel(tc, assign, xp_bytes, xp_scale, codebook, out):
 
     chunks = []
     for b in range(B):
-        c0 = 0
-        for w in WIDTHS[b]:
-            for g in range(PASSES):
+        for g in range(PASSES):
+            c0 = 0
+            for w in WIDTHS[b][g]:
                 chunks.append((b, g, c0, w))
-            c0 += w
+                c0 += w
     n_chunks = len(chunks)
+
+    def ranges_of(i):
+        b, g, c0, w = chunks[i]
+        found = []
+        r0 = 0
+        for rw in RANGES[b]:
+            if c0 <= r0 < c0 + w:
+                found.append((r0, rw))
+            r0 += rw
+        return found
 
     with ExitStack() as ctx:
         keep = ctx.enter_context(tc.tile_pool(name="keep", bufs=1))
-        widep = ctx.enter_context(tc.tile_pool(name="widep", bufs=4))
-        grpp = ctx.enter_context(tc.tile_pool(name="grpp", bufs=3))
-        outp = ctx.enter_context(tc.tile_pool(name="outp", bufs=4))
-        psum = ctx.enter_context(tc.psum_pool(name="psum", bufs=6))
-        psum1 = ctx.enter_context(tc.psum_pool(name="psum1", bufs=1))
+        wide_pool = ctx.enter_context(tc.tile_pool(name="wide_pool", bufs=4))
+        grouped_pool = ctx.enter_context(tc.tile_pool(name="grouped_pool", bufs=3))
+        out_pool = ctx.enter_context(tc.tile_pool(name="out_pool", bufs=4))
+        acc_pool = ctx.enter_context(tc.psum_pool(name="acc_pool", bufs=6))
+        asum_pool = ctx.enter_context(tc.psum_pool(name="asum_pool", bufs=1))
         ctx.enter_context(tc.manual_schedule())
 
-        xs = keep.tile([P, PASSES, PACK], F32, name="xs")
-        nc.scalar.dma_start(out=xs[:], in_=xp_scale[0, :, 0].rearrange("(g p t) -> p g t", p=P, t=PACK))
+        x_scale = keep.tile([P, PASSES, PACK], F32, name="x_scale")
+        nc.scalar.dma_start(out=x_scale[:], in_=xp_scale[0, :, 0].rearrange("(g p t) -> p g t", p=P, t=PACK))
 
-        xbytes = []
+        x_bytes = []
         for u in range(B * PASSES):
-            xb = keep.tile([P, PACK, C], U8, name="xbytes%d" % u)
-            xbytes.append(xb)
+            x_bytes_u = keep.tile([P, PACK, C], U8, name="x_bytes%d" % u)
+            x_bytes.append(x_bytes_u)
 
-        def load_bytes(b, g, t0, t1, c0, w):
-            src = xp_bytes[b, g * K_PASS:(g + 1) * K_PASS, c0:c0 + w].rearrange("(p t) c -> p t c", t=PACK)
-            nc.sync.dma_start(out=xbytes[b * PASSES + g][:, t0:t1, c0:c0 + w], in_=src[:, t0:t1, :])
+        def load_bytes(b, g, t0, t1):
+            src = xp_bytes[b, g * K_PASS:(g + 1) * K_PASS, :].rearrange("(p t) c -> p t c", t=PACK)
+            nc.sync.dma_start(out=x_bytes[b * PASSES + g][:, t0:t1, :], in_=src[:, t0:t1, :])
 
+        for t in range(PACK):
+            load_bytes(0, 0, t, t + 1)
+        load_bytes(0, 1, 0, PACK)
         a_raw = keep.tile([P, B * PASSES, PACK, K], BF16, name="a_raw")
-        a_view = assign.rearrange("b (g p t) k -> p (b g) (t k)", p=P, t=PACK)
-
-        def load_assign(n0, n1):
-            nc.sync.dma_start(out=a_raw[:, n0:n1, :, :].rearrange("p n t k -> p n (t k)"), in_=a_view[:, n0:n1, :])
-
-        for g in range(PASSES):
-            for t in range(PACK):
-                load_bytes(0, g, t, t + 1, 0, C)
-        load_assign(0, B * PASSES)
-        cb = keep.tile([P, C], BF16, name="cb")
-        nc.sync.dma_start(out=cb[:], in_=codebook)
+        nc.sync.dma_start(
+            out=a_raw[:].rearrange("p n t k -> p n (t k)"),
+            in_=assign.rearrange("b (g p t) k -> p (b g) (t k)", p=P, t=PACK),
+        )
+        codebook_sb = keep.tile([P, C], BF16, name="codebook_sb")
+        nc.sync.dma_start(out=codebook_sb[:], in_=codebook)
         for b in range(1, B):
             for g in range(PASSES):
-                load_bytes(b, g, 0, PACK, 0, C)
+                load_bytes(b, g, 0, PACK)
 
         neg_ones = keep.tile([P, 1], BF16, name="neg_ones")
         nc.gpsimd.memset(neg_ones[:], -1.0)
@@ -86,81 +98,14 @@ def tile_lvc_pb_kernel(tc, assign, xp_bytes, xp_scale, codebook, out):
         a_grouped = keep.tile([P, B * PASSES, K, PACK], BF16, name="a_grouped", align_bytes=64)
         a_codes = keep.tile([P, B * PASSES * K], U32, name="a_codes", align_bytes=64)
         a_planes = keep.tile([P, B * PASSES * K], U8, name="a_planes", align_bytes=64)
-        asum_ps = psum1.tile([P, B], F32, name="asum_ps")
+        neg_asum_ps = asum_pool.tile([P, B], F32, name="neg_asum_ps")
         neg_asum = keep.tile([P, B], F32, name="neg_asum")
 
-        wide = {}
-        grouped = {}
-        codes = {}
-        planes = {}
-        acc = {}
-
-        def widen(i):
-            b, g, c0, w = chunks[i]
-            wt = widep.tile([P, PACK, w], BF16, name="wide")
-            wide[i] = wt
-            for t in range(PACK):
-                src = xbytes[b * PASSES + g][:, t, c0:c0 + w].bitcast(FP8)
-                if (i, t) in V_WIDENS:
-                    nc.vector.tensor_scalar(out=wt[:, t, :], in0=src, scalar1=xs[:, g, t:t + 1], scalar2=None, op0=MULT)
-                else:
-                    nc.scalar.activation(out=wt[:, t, :], in_=src, func=COPY, scale=xs[:, g, t:t + 1])
-
-        def interleave(i):
-            w = chunks[i][3]
-            gt = grpp.tile([P, w, PACK], BF16, name="grouped", align_bytes=64)
-            grouped[i] = gt
-            if i in S_INTERLEAVES:
-                nc.scalar.copy(out=gt[:], in_=wide[i][:].rearrange("p t c -> p c t"))
-            else:
-                nc.vector.tensor_copy(
-                    out=gt[:].rearrange("p (c j) t -> p c t j", j=RUN),
-                    in_=wide[i][:].rearrange("p t (c j) -> p c t j", j=RUN),
-                )
-
-        def quantize(i):
-            w = chunks[i][3]
-            xc = keep.tile([P, w], U32, name="codes%d" % i, align_bytes=64)
-            xpl = keep.tile([P, w], U8, name="planes%d" % i, align_bytes=64)
-            codes[i] = xc
-            planes[i] = xpl
-            nc.vector.quantize_mx(
-                out=xc[:].bitcast(FP8X4), scales=xpl[:], in_=grouped[i][:].rearrange("p c t -> p (c t)")
-            )
-
-        def multiply(i):
-            b, g, c0, w = chunks[i]
-            a_cols = slice((b * PASSES + g) * K, (b * PASSES + g + 1) * K)
-            for d in range(0, w, BANK):
-                n = min(w, BANK)
-                if g == 0:
-                    acc_t = psum.tile([P, n], F32, name="acc")
-                    acc[(b, c0 + d)] = acc_t
-                nc.tensor.matmul_mx(
-                    out=acc[(b, c0 + d)][:],
-                    lhsT=a_codes[:, a_cols].bitcast(FP8X4),
-                    lhsT_scale=a_planes[:, a_cols],
-                    rhs=codes[i][:, d:d + n].bitcast(FP8X4),
-                    rhs_scale=planes[i][:, d:d + n],
-                    start=(g == 0),
-                    stop=(g == PASSES - 1),
-                )
-
-        def finish(i):
-            b, g, c0, w = chunks[i]
-            for d in range(c0, c0 + w, BANK):
-                n = min(w, BANK)
-                ot = outp.tile([P, n], F32, name="ot")
-                nc.vector.scalar_tensor_tensor(
-                    out=ot[:], in0=cb[:, d:d + n], scalar=neg_asum[:, b:b + 1], in1=acc[(b, d)][:], op0=MULT, op1=ADD
-                )
-                nc.sync.dma_start(out=out[b, :, d:d + n], in_=ot[:])
-
-        def assign_sums(b0, b1):
-            for b in range(b0, b1):
+        def assign_sums():
+            for b in range(B):
                 for j in range(PASSES * PACK):
                     nc.tensor.matmul(
-                        out=asum_ps[:, b:b + 1],
+                        out=neg_asum_ps[:, b:b + 1],
                         lhsT=a_raw[:, b * PASSES + j // PACK, j % PACK, :],
                         rhs=neg_ones[:],
                         start=(j == 0),
@@ -175,11 +120,82 @@ def tile_lvc_pb_kernel(tc, assign, xp_bytes, xp_scale, codebook, out):
                 out=a_codes[:].bitcast(FP8X4), scales=a_planes[:], in_=a_grouped[:].rearrange("p n k t -> p (n k t)")
             )
 
+        wide = {}
+        grouped = {}
+        codes = {}
+        planes = {}
+        acc = {}
+
+        def widen(i):
+            b, g, c0, w = chunks[i]
+            wide_i = wide_pool.tile([P, PACK, w], BF16, name="wide")
+            wide[i] = wide_i
+            for t in range(PACK):
+                src = x_bytes[b * PASSES + g][:, t, c0:c0 + w].bitcast(FP8)
+                scale_col = x_scale[:, g, t:t + 1]
+                if (i, t) in V_WIDENS:
+                    nc.vector.tensor_scalar(out=wide_i[:, t, :], in0=src, scalar1=scale_col, scalar2=None, op0=MULT)
+                else:
+                    nc.scalar.activation(out=wide_i[:, t, :], in_=src, func=COPY, scale=scale_col)
+
+        def interleave(i):
+            w = chunks[i][3]
+            grouped_i = grouped_pool.tile([P, w, PACK], BF16, name="grouped", align_bytes=64)
+            grouped[i] = grouped_i
+            if i in S_INTERLEAVES:
+                nc.scalar.copy(out=grouped_i[:], in_=wide[i][:].rearrange("p t c -> p c t"))
+            else:
+                nc.vector.tensor_copy(
+                    out=grouped_i[:].rearrange("p (c j) t -> p c t j", j=RUN),
+                    in_=wide[i][:].rearrange("p t (c j) -> p c t j", j=RUN),
+                )
+
+        def quantize(i):
+            w = chunks[i][3]
+            codes_i = keep.tile([P, w], U32, name="codes%d" % i, align_bytes=64)
+            planes_i = keep.tile([P, w], U8, name="planes%d" % i, align_bytes=64)
+            codes[i] = codes_i
+            planes[i] = planes_i
+            nc.vector.quantize_mx(
+                out=codes_i[:].bitcast(FP8X4), scales=planes_i[:], in_=grouped[i][:].rearrange("p c t -> p (c t)")
+            )
+
+        def multiply(i):
+            b, g, c0, w = chunks[i]
+            a_cols = slice((b * PASSES + g) * K, (b * PASSES + g + 1) * K)
+            for r0, rw in ranges_of(i):
+                if g == 0:
+                    acc_br = acc_pool.tile([P, rw], F32, name="acc")
+                    acc[(b, r0)] = acc_br
+                nc.tensor.matmul_mx(
+                    out=acc[(b, r0)][:],
+                    lhsT=a_codes[:, a_cols].bitcast(FP8X4),
+                    lhsT_scale=a_planes[:, a_cols],
+                    rhs=codes[i][:, r0 - c0:r0 - c0 + rw].bitcast(FP8X4),
+                    rhs_scale=planes[i][:, r0 - c0:r0 - c0 + rw],
+                    start=(g == 0),
+                    stop=(g == PASSES - 1),
+                )
+
+        def finish(i):
+            b = chunks[i][0]
+            for r0, rw in ranges_of(i):
+                result = out_pool.tile([P, rw], F32, name="result")
+                nc.vector.scalar_tensor_tensor(
+                    out=result[:],
+                    in0=codebook_sb[:, r0:r0 + rw],
+                    scalar=neg_asum[:, b:b + 1],
+                    in1=acc[(b, r0)][:],
+                    op0=MULT,
+                    op1=ADD,
+                )
+                nc.sync.dma_start(out=out[b, :, r0:r0 + rw], in_=result[:])
+
         widen(0)
         widen(1)
         interleave(0)
         assign_interleave()
-        assign_sums(0, B)
+        assign_sums()
         closed = []
         for i in range(n_chunks):
             if i + 1 in S_INTERLEAVES:
@@ -191,7 +207,7 @@ def tile_lvc_pb_kernel(tc, assign, xp_bytes, xp_scale, codebook, out):
             quantize(i)
             if i == 0:
                 assign_quantize()
-                nc.vector.tensor_copy(out=neg_asum[:], in_=asum_ps[:])
+                nc.vector.tensor_copy(out=neg_asum[:], in_=neg_asum_ps[:])
             for j in closed:
                 finish(j)
             closed = []

@@ -24,7 +24,7 @@ WIDTHS = (((1024,), (1024,)), ((1024,), (1024,)), ((1024,), (1024,)), ((1024,), 
 
 RANGES = ((512, 512), (512, 512), (512, 512), (512, 256, 256))
 
-V_WIDENS = ((0, 1), (0, 2), (0, 3))
+V_WIDENS = ((0, 1), (0, 2), (0, 3), (1, 3))
 
 S_INTERLEAVES = (7, 9)
 

@@ -76,7 +76,9 @@ def tile_lvc_pb_kernel(tc, assign, xp_bytes, xp_scale, codebook, out):
 
         for t in range(PACK):
             load_bytes(0, 0, t, t + 1)
-        load_bytes(0, 1, 0, PACK)
+        load_bytes(0, 1, 0, 1)
+        load_bytes(0, 1, 1, PACK)
+        load_bytes(1, 0, 0, PACK)
         a_raw = keep.tile([P, B * PASSES, PACK, K], BF16, name="a_raw")
         nc.sync.dma_start(
             out=a_raw[:].rearrange("p n t k -> p n (t k)"),
@@ -86,7 +88,8 @@ def tile_lvc_pb_kernel(tc, assign, xp_bytes, xp_scale, codebook, out):
         nc.sync.dma_start(out=codebook_sb[:], in_=codebook)
         for b in range(1, B):
             for g in range(PASSES):
-                load_bytes(b, g, 0, PACK)
+                if (b, g) != (1, 0):
+                    load_bytes(b, g, 0, PACK)
 
         neg_ones = keep.tile([P, 1], BF16, name="neg_ones")
         nc.gpsimd.memset(neg_ones[:], -1.0)
@@ -194,8 +197,6 @@ def tile_lvc_pb_kernel(tc, assign, xp_bytes, xp_scale, codebook, out):
         widen(0)
         widen(1)
         interleave(0)
-        assign_interleave()
-        assign_sums()
         closed = []
         for i in range(n_chunks):
             if i + 1 in S_INTERLEAVES:
@@ -204,6 +205,9 @@ def tile_lvc_pb_kernel(tc, assign, xp_bytes, xp_scale, codebook, out):
                 widen(i + 2)
             if i + 1 < n_chunks and i + 1 not in S_INTERLEAVES:
                 interleave(i + 1)
+            if i == 0:
+                assign_interleave()
+                assign_sums()
             quantize(i)
             if i == 0:
                 assign_quantize()

@@ -212,9 +212,10 @@ def tile_lvc_pb_kernel(tc, assign, xp_bytes, xp_scale, codebook, out):
             if i == 0:
                 assign_quantize()
                 nc.vector.tensor_copy(out=neg_asum[:], in_=neg_asum_ps[:])
-            for j in closed:
-                finish(j)
-            closed = []
+            if i != n_chunks - 2:
+                for j in closed:
+                    finish(j)
+                closed = []
             multiply(i)
             if chunks[i][1] == PASSES - 1:
                 closed.append(i)

@@ -29,6 +29,7 @@ V_WIDENS = ((0, 1), (0, 2), (0, 3), (1, 3))
 S_INTERLEAVES = (7, 9)
 
 RUN = 4
+PORTS = 2
 
 
 def tile_lvc_pb_kernel(tc, assign, xp_bytes, xp_scale, codebook, out):
@@ -146,11 +147,14 @@ def tile_lvc_pb_kernel(tc, assign, xp_bytes, xp_scale, codebook, out):
             grouped_i = grouped_pool.tile([P, w, PACK], BF16, name="grouped", align_bytes=64)
             grouped[i] = grouped_i
             if i in S_INTERLEAVES:
-                nc.scalar.copy(out=grouped_i[:], in_=wide[i][:].rearrange("p t c -> p c t"))
-            else:
-                nc.vector.tensor_copy(
+                nc.scalar.copy(
                     out=grouped_i[:].rearrange("p (c j) t -> p c t j", j=RUN),
                     in_=wide[i][:].rearrange("p t (c j) -> p c t j", j=RUN),
+                )
+            else:
+                nc.vector.tensor_copy(
+                    out=grouped_i[:].rearrange("p (c h j) t -> p h c t j", h=PORTS, j=RUN),
+                    in_=wide[i][:].rearrange("p t (c h j) -> p h c t j", h=PORTS, j=RUN),
                 )
 
         def quantize(i):

@@ -64,7 +64,7 @@ def tile_lvc_pb_kernel(tc, assign, xp_bytes, xp_scale, codebook, out):
         ctx.enter_context(tc.manual_schedule())
 
         x_scale = keep.tile([P, PASSES, PACK], F32, name="x_scale")
-        nc.scalar.dma_start(out=x_scale[:], in_=xp_scale[0, :, 0].rearrange("(g p t) -> p g t", p=P, t=PACK))
+        nc.sync.dma_start(out=x_scale[:], in_=xp_scale[0, :, 0].rearrange("(g p t) -> p g t", p=P, t=PACK))
 
         x_bytes = []
         for u in range(B * PASSES):

from contextlib import ExitStack

import concourse.mybir as mybir

B, NPIX, C, K = 4, 1024, 1024, 128
FLOPS = 2 * B * K * NPIX * C

F32 = mybir.dt.float32
BF16 = mybir.dt.bfloat16
U32 = mybir.dt.uint32
U8 = mybir.dt.uint8
FP8 = mybir.dt.float8_e4m3fn
FP8X4 = mybir.dt.float8_e4m3fn_x4
COPY = mybir.ActivationFunctionType.Copy
MULT = mybir.AluOpType.mult
ADD = mybir.AluOpType.add

P = 128
PACK = 4
K_PASS = P * PACK
PASSES = NPIX // K_PASS

WIDTHS = (((1024,), (1024,)), ((1024,), (1024,)), ((1024,), (1024,)), ((1024,), (512, 256, 256)))

RANGES = ((512, 512), (512, 512), (512, 512), (512, 256, 256))

V_WIDENS = ((0, 1), (0, 2), (0, 3), (1, 3))

S_INTERLEAVES = (7, 9)

RUN = 4
PORTS = 2


def tile_lvc_pb_kernel(tc, assign, xp_bytes, xp_scale, codebook, out):
    nc = tc.nc

    chunks = []
    for b in range(B):
        for g in range(PASSES):
            c0 = 0
            for w in WIDTHS[b][g]:
                chunks.append((b, g, c0, w))
                c0 += w
    n_chunks = len(chunks)

    def ranges_of(i):
        b, g, c0, w = chunks[i]
        found = []
        r0 = 0
        for rw in RANGES[b]:
            if c0 <= r0 < c0 + w:
                found.append((r0, rw))
            r0 += rw
        return found

    with ExitStack() as ctx:
        keep = ctx.enter_context(tc.tile_pool(name="keep", bufs=1))
        wide_pool = ctx.enter_context(tc.tile_pool(name="wide_pool", bufs=4))
        grouped_pool = ctx.enter_context(tc.tile_pool(name="grouped_pool", bufs=3))
        out_pool = ctx.enter_context(tc.tile_pool(name="out_pool", bufs=4))
        acc_pool = ctx.enter_context(tc.psum_pool(name="acc_pool", bufs=6))
        asum_pool = ctx.enter_context(tc.psum_pool(name="asum_pool", bufs=1))
        ctx.enter_context(tc.manual_schedule())

        x_scale = keep.tile([P, PASSES, PACK], F32, name="x_scale")
        nc.sync.dma_start(out=x_scale[:], in_=xp_scale[0, :, 0].rearrange("(g p t) -> p g t", p=P, t=PACK))

        x_bytes = []
        for u in range(B * PASSES):
            x_bytes_u = keep.tile([P, PACK, C], U8, name="x_bytes%d" % u)
            x_bytes.append(x_bytes_u)

        def load_bytes(b, g, t0, t1):
            src = xp_bytes[b, g * K_PASS:(g + 1) * K_PASS, :].rearrange("(p t) c -> p t c", t=PACK)
            nc.sync.dma_start(out=x_bytes[b * PASSES + g][:, t0:t1, :], in_=src[:, t0:t1, :])

        for t in range(PACK):
            load_bytes(0, 0, t, t + 1)
        load_bytes(0, 1, 0, 1)
        load_bytes(0, 1, 1, PACK)
        load_bytes(1, 0, 0, PACK)
        a_raw = keep.tile([P, B * PASSES, PACK, K], BF16, name="a_raw")
        nc.sync.dma_start(
            out=a_raw[:].rearrange("p n t k -> p n (t k)"),
            in_=assign.rearrange("b (g p t) k -> p (b g) (t k)", p=P, t=PACK),
        )
        codebook_sb = keep.tile([P, C], BF16, name="codebook_sb")
        nc.sync.dma_start(out=codebook_sb[:], in_=codebook)
        for b in range(1, B):
            for g in range(PASSES):
                if (b, g) != (1, 0):
                    load_bytes(b, g, 0, PACK)

        neg_ones = keep.tile([P, 1], BF16, name="neg_ones")
        nc.gpsimd.memset(neg_ones[:], -1.0)
        warm_in = keep.tile([P, 1], F32, name="warm_in")
        warm_out = keep.tile([P, 1], F32, name="warm_out")
        nc.gpsimd.memset(warm_in[:], 0.0)
        nc.scalar.activation(out=warm_out[:], in_=warm_in[:], func=COPY)

        a_grouped = keep.tile([P, B * PASSES, K, PACK], BF16, name="a_grouped", align_bytes=64)
        a_codes = keep.tile([P, B * PASSES * K], U32, name="a_codes", align_bytes=64)
        a_planes = keep.tile([P, B * PASSES * K], U8, name="a_planes", align_bytes=64)
        neg_asum_ps = asum_pool.tile([P, B], F32, name="neg_asum_ps")
        neg_asum = keep.tile([P, B], F32, name="neg_asum")

        def assign_sums():
            for b in range(B):
                for j in range(PASSES * PACK):
                    nc.tensor.matmul(
                        out=neg_asum_ps[:, b:b + 1],
                        lhsT=a_raw[:, b * PASSES + j // PACK, j % PACK, :],
                        rhs=neg_ones[:],
                        start=(j == 0),
                        stop=(j == PASSES * PACK - 1),
                    )

        def assign_interleave():
            nc.vector.tensor_copy(out=a_grouped[:], in_=a_raw[:].rearrange("p n t k -> p n k t"))

        def assign_quantize():
            nc.vector.quantize_mx(
                out=a_codes[:].bitcast(FP8X4), scales=a_planes[:], in_=a_grouped[:].rearrange("p n k t -> p (n k t)")
            )

        wide = {}
        grouped = {}
        codes = {}
        planes = {}
        acc = {}

        def widen(i):
            b, g, c0, w = chunks[i]
            wide_i = wide_pool.tile([P, PACK, w], BF16, name="wide")
            wide[i] = wide_i
            for t in range(PACK):
                src = x_bytes[b * PASSES + g][:, t, c0:c0 + w].bitcast(FP8)
                scale_col = x_scale[:, g, t:t + 1]
                if (i, t) in V_WIDENS:
                    nc.vector.tensor_scalar(out=wide_i[:, t, :], in0=src, scalar1=scale_col, scalar2=None, op0=MULT)
                else:
                    nc.scalar.activation(out=wide_i[:, t, :], in_=src, func=COPY, scale=scale_col)

        def interleave(i):
            w = chunks[i][3]
            grouped_i = grouped_pool.tile([P, w, PACK], BF16, name="grouped", align_bytes=64)
            grouped[i] = grouped_i
            if i in S_INTERLEAVES:
                nc.scalar.copy(
                    out=grouped_i[:].rearrange("p (c j) t -> p c t j", j=RUN),
                    in_=wide[i][:].rearrange("p t (c j) -> p c t j", j=RUN),
                )
            else:
                nc.vector.tensor_copy(
                    out=grouped_i[:].rearrange("p (c h j) t -> p h c t j", h=PORTS, j=RUN),
                    in_=wide[i][:].rearrange("p t (c h j) -> p h c t j", h=PORTS, j=RUN),
                )

        def quantize(i):
            w = chunks[i][3]
            codes_i = keep.tile([P, w], U32, name="codes%d" % i, align_bytes=64)
            planes_i = keep.tile([P, w], U8, name="planes%d" % i, align_bytes=64)
            codes[i] = codes_i
            planes[i] = planes_i
            nc.vector.quantize_mx(
                out=codes_i[:].bitcast(FP8X4), scales=planes_i[:], in_=grouped[i][:].rearrange("p c t -> p (c t)")
            )

        def multiply(i):
            b, g, c0, w = chunks[i]
            a_cols = slice((b * PASSES + g) * K, (b * PASSES + g + 1) * K)
            for r0, rw in ranges_of(i):
                if g == 0:
                    acc_br = acc_pool.tile([P, rw], F32, name="acc")
                    acc[(b, r0)] = acc_br
                nc.tensor.matmul_mx(
                    out=acc[(b, r0)][:],
                    lhsT=a_codes[:, a_cols].bitcast(FP8X4),
                    lhsT_scale=a_planes[:, a_cols],
                    rhs=codes[i][:, r0 - c0:r0 - c0 + rw].bitcast(FP8X4),
                    rhs_scale=planes[i][:, r0 - c0:r0 - c0 + rw],
                    start=(g == 0),
                    stop=(g == PASSES - 1),
                )

        def finish(i):
            b = chunks[i][0]
            for r0, rw in ranges_of(i):
                result = out_pool.tile([P, rw], F32, name="result")
                nc.vector.scalar_tensor_tensor(
                    out=result[:],
                    in0=codebook_sb[:, r0:r0 + rw],
                    scalar=neg_asum[:, b:b + 1],
                    in1=acc[(b, r0)][:],
                    op0=MULT,
                    op1=ADD,
                )
                nc.sync.dma_start(out=out[b, :, r0:r0 + rw], in_=result[:])

        widen(0)
        widen(1)
        interleave(0)
        closed = []
        for i in range(n_chunks):
            if i + 1 in S_INTERLEAVES:
                interleave(i + 1)
            if i + 2 < n_chunks:
                widen(i + 2)
            if i + 1 < n_chunks and i + 1 not in S_INTERLEAVES:
                interleave(i + 1)
            if i == 0:
                assign_interleave()
                assign_sums()
            quantize(i)
            if i == 0:
                assign_quantize()
                nc.vector.tensor_copy(out=neg_asum[:], in_=neg_asum_ps[:])
            if i != n_chunks - 2:
                for j in closed:
                    finish(j)
                closed = []
            multiply(i)
            if chunks[i][1] == PASSES - 1:
                closed.append(i)
        for j in closed:
            finish(j)
